import numpy as np
import ml_dtypes


def mxq(x, axis, fmt="e4m3"):
    dtype, down = {"e4m3": (ml_dtypes.float8_e4m3fn, 7), "e5m2": (ml_dtypes.float8_e5m2, 14)}[fmt]
    v = np.moveaxis(np.asarray(x, np.float32).astype(ml_dtypes.bfloat16).astype(np.float64), axis, -1)
    blocks = v.reshape(v.shape[:-1] + (-1, 32))
    amax = np.abs(blocks).max(-1, keepdims=True)
    byte = np.maximum(np.where(amax > 0, np.frexp(amax)[1] - 1 + 127, 0) - down, 1)
    scale = np.exp2(byte - 127.0)
    codes = (blocks / scale).astype(np.float32).astype(dtype).astype(np.float64)
    return np.moveaxis((codes * scale).reshape(v.shape), -1, axis)


WIDE = False


def mx_kscale(k):
    if not WIDE:
        return np.ones(k)
    levels = np.array([10, -10, 5, -5, 0])
    if k % 512:
        return np.exp2(np.random.permutation(np.resize(levels, k // 32))).repeat(32)
    a = np.empty((k // 512, 16))
    for p in range(k // 512):
        a[p, :8] = np.random.permutation(np.resize(levels, 8))
        for g in range(8):
            far = levels[np.abs(levels - a[p, g]) >= 10]
            a[p, g + 8] = far[np.random.randint(len(far))]
    return np.exp2(a.ravel()).repeat(32)


BF16 = ml_dtypes.bfloat16


def bf(x):
    return np.asarray(x, np.float32).astype(BF16)


def f64(x):
    return np.asarray(x).astype(np.float64)


NK, F, B = 3072, 512, 512
D = 2 * F
EPS = 1e-8


def rotate_half(x):
    d = x.shape[-1] // 2
    return np.concatenate([-x[..., d:], x[..., :d]], axis=-1)


def setup_inputs():
    s = mx_kscale(NK)[:, None]
    u = mx_kscale(B)
    K0 = bf(np.random.standard_normal((NK, D)))
    ang = bf(np.random.random(F) * 2.0 * np.pi)
    probes0 = bf(np.random.standard_normal((B, D)))
    uw0 = bf(np.random.standard_normal((B, F)) * 0.5 / np.sqrt(F))
    k_bias = bf(np.random.standard_normal(B) * 0.5)
    g = bf(np.random.standard_normal((NK, B)) * np.exp2(np.random.randint(-6, 1, (NK, 1))) * 4.0 / s * u)
    rnorm = 1.0 / (np.sqrt(np.sum(f64(probes0) ** 2, axis=-1, keepdims=True)) + EPS)
    return {"K": bf(f64(K0) * s),
            "reference_angles": ang,
            "probes": bf(f64(probes0) / u[:, None]),
            "u_weights": bf(f64(uw0) / u[:, None]),
            "k_bias": k_bias,
            "rnorm": np.asarray(rnorm, np.float32),
            "grad_out": g}


def reference(K, reference_angles, probes, u_weights, k_bias, rnorm, grad_out):
    K = f64(K)
    probes = f64(probes)
    r = f64(rnorm)
    g = f64(grad_out)
    theta = np.concatenate([f64(reference_angles), f64(reference_angles)], axis=-1)
    c = np.cos(theta)
    sn = np.sin(theta)
    p = probes * r
    rotated = p * c + rotate_half(p) * sn
    W = np.concatenate([rotated, f64(u_weights)], axis=1)
    dX = mxq(g, 1, "e5m2") @ mxq(W, 0, "e4m3")
    K_mag = np.sqrt(K[:, :F] ** 2 + K[:, F:] ** 2 + EPS)
    q = dX[:, D:] / K_mag
    dK = dX[:, :D] + K * np.concatenate([q, q], axis=1)
    G = mxq(g, 0, "e5m2").T @ mxq(K, 0, "e4m3")
    dp = G * c - rotate_half(G) * sn
    dot = np.sum(dp * probes, axis=1, keepdims=True)
    dprobes = dp * r - probes * dot * r ** 3 / (1.0 - EPS * r)
    return dK, dprobes

import math
from contextlib import ExitStack

import concourse.mybir as mybir
from concourse.masks import make_identity

NK, F, B = 3072, 512, 512
D = 2 * F
EPS = 1e-8
FLOPS = 2 * NK * B * (D + F) + 2 * NK * B * D
BYTES = 2 * (NK * D + F + B * D + B * F + NK * B) + 4 * (B + NK * D + B * D)

F32 = mybir.dt.float32
BF16 = mybir.dt.bfloat16
I32 = mybir.dt.int32
U32 = mybir.dt.uint32
U8 = mybir.dt.uint8
E4 = mybir.dt.float8_e4m3fn_x4
E5 = mybir.dt.float8_e5m2_x4
ALU = mybir.AluOpType
ACT = mybir.ActivationFunctionType

P = 128
PACK = 4
CHUNK = P * PACK
NCHUNK = NK // CHUNK
NTILE = NK // P
CFG = {'start': [0, 0, 3, 4, 7, 10], 'sk': [1, 2, 2, 2, 2, 3], 'sg': [0, 2, 3, 3, 3, 4], 'su': 0, 'sr': 1, 'g0': 13, 'gs': 3, 'd0': 6, 'pe': [1, 1, 1, 1, 1, 1, 0, 1, 1, 1, 1, 1, 1, 1, 0, 1, 0, 0, 0, 0, 1, 1, 1, 1], 'kb': 2}


def tile_module2network_v_kernel(
    tc, K, reference_angles, probes, u_weights, k_bias, rnorm, grad_out, out_0, out_1
):
    nc = tc.nc
    K_hbm = K.rearrange("(g p j) w -> p g j w", p=P, j=PACK)
    g_hbm = grad_out.rearrange("(g p j) w -> p g j w", p=P, j=PACK)
    o0_hbm = out_0.rearrange("(g p j) w -> p g j w", p=P, j=PACK)
    o1_hbm = out_1.rearrange("(p j) w -> p j w", j=PACK)

    with ExitStack() as ctx:
        keep = ctx.enter_context(tc.tile_pool(name="keep", bufs=1))
        work = ctx.enter_context(tc.tile_pool(name="work", bufs=2))
        psum = ctx.enter_context(tc.psum_pool(name="psum", bufs=1))

        theta = keep.tile([P, F], BF16, name="theta")
        nc.scalar.dma_start(out=theta[:], in_=reference_angles.partition_broadcast(P))
        r = keep.tile([P, PACK], F32, name="r")
        nc.scalar.dma_start(out=r[:], in_=rnorm.rearrange("(p j) o -> p (j o)", j=PACK))
        probes_sb = keep.tile([P, PACK, D], BF16, name="probes_sb")
        u_raw = keep.tile([P, PACK, F], BF16, name="u_raw")
        g_raw, K_raw = [], []
        for c in range(NCHUNK):
            g_c = keep.tile([P, PACK, B], BF16, name="g_c", tag="g_raw", bufs=4, align_bytes=64)
            nc.sync.dma_start(out=g_c[:], in_=g_hbm[:, c, :, :])
            g_raw.append(g_c)
            if c == 0:
                nc.sync.dma_start(out=probes_sb[:], in_=probes.rearrange("(p j) w -> p j w", j=PACK))
                nc.sync.dma_start(out=u_raw[:], in_=u_weights.rearrange("(p j) w -> p j w", j=PACK))
            K_c = keep.tile([P, PACK, D], BF16, name="K_c", tag="K_raw", bufs=NCHUNK, align_bytes=64)
            nc.sync.dma_start(out=K_c[:], in_=K_hbm[:, c, :, :])
            K_raw.append(K_c)

        ident = keep.tile([P, P], F32, name="ident")
        make_identity(nc, ident[:])

        g_codes = keep.tile([P, NCHUNK, B], U32, name="g_codes", align_bytes=64)
        g_scales = keep.tile([P, NCHUNK, B], U8, name="g_scales", align_bytes=64)
        K_codes = keep.tile([P, NCHUNK, D], U32, name="K_codes", align_bytes=64)
        K_scales = keep.tile([P, NCHUNK, D], U8, name="K_scales", align_bytes=64)
        rot_codes = keep.tile([P, D], U32, name="rot_codes", align_bytes=64)
        rot_scales = keep.tile([P, D], U8, name="rot_scales", align_bytes=64)
        u_codes = keep.tile([P, F], U32, name="u_codes", align_bytes=64)
        u_scales = keep.tile([P, F], U8, name="u_scales", align_bytes=64)
        rot_bf = keep.tile([P, PACK, D], BF16, name="rot_bf", align_bytes=64)
        cs = keep.tile([P, F], F32, name="cs")
        sn = keep.tile([P, F], F32, name="sn")
        c_col = keep.tile([P, PACK], F32, name="c_col")
        s_col = keep.tile([P, PACK], F32, name="s_col")
        ns_col = keep.tile([P, PACK], F32, name="ns_col")
        w_norm = keep.tile([P, PACK], F32, name="w_norm")
        small = keep.tile([P, PACK], F32, name="small")
        dots = keep.tile([P, 2 * PACK], F32, name="dots")

        def flat(t):
            return t[:].rearrange("p w j -> p (w j)")

        def interleave(engine_copy, dst, src, lo, hi):
            engine_copy(
                out=dst[:, lo:hi, :].rearrange("p (c i) t -> p c t i", i=4),
                in_=src[:, :, lo:hi].rearrange("p t (c i) -> p c t i", i=4),
            )

        xt, gT_st, gT_codes, gT_scales = {}, {}, {}, {}

        def g_transpose(c, h):
            xt[c, h] = psum.tile([P, 2, 2, P], F32, name="xt", tag="xt")
            for a in range(2):
                words = g_raw[c][:, 2 * h + a, :].bitcast(F32)
                for u in range(2):
                    nc.tensor.transpose(xt[c, h][:, a, u, :], words[:, u::2], ident[:])

        def g_transpose_out(c, h):
            if h == 0:
                gT_st[c] = work.tile([P, CHUNK, PACK], BF16, name="gT_st", tag="gst", bufs=3, align_bytes=64)
            words = flat(gT_st[c]).bitcast(F32)[:, 512 * h : 512 * (h + 1)]
            nc.scalar.copy(
                out=words.rearrange("p (a r u) -> p a r u", a=2, u=2),
                in_=xt[c, h][:].rearrange("p a u r -> p a r u"),
            )

        def gT_quant(c):
            gT_codes[c] = work.tile([P, CHUNK], U32, name="gT_codes", tag="gT_codes", bufs=3, align_bytes=64)
            gT_scales[c] = work.tile([P, CHUNK], U8, name="gT_scales", tag="gT_scales", bufs=3, align_bytes=64)
            nc.vector.quantize_mx(out=gT_codes[c][:].bitcast(E5), scales=gT_scales[c][:], in_=flat(gT_st[c]))

        g_st = {}

        def g_interleave(c, engine_copy, t0, t1):
            if c not in g_st:
                g_st[c] = work.tile([P, B, PACK], BF16, name="g_st", tag="gst", bufs=3, align_bytes=64)
            engine_copy(
                out=flat(g_st[c]).rearrange("p (t m j) -> p t m j", t=4, j=4)[:, t0:t1, :, :],
                in_=g_raw[c][:].rearrange("p j (m t) -> p t m j", t=4)[:, t0:t1, :, :],
            )

        def g_quant(c):
            nc.vector.quantize_mx(out=g_codes[:, c, :].bitcast(E5), scales=g_scales[:, c, :], in_=flat(g_st[c]))

        K_st = {}

        def K_interleave(c, engine_copy, k0, k1):
            if c not in K_st:
                K_st[c] = work.tile([P, D, PACK], BF16, name="K_st", tag="wide", bufs=CFG["kb"], align_bytes=64)
            interleave(engine_copy, K_st[c], K_raw[c], 256 * k0, 256 * k1)

        def K_quant(c):
            nc.vector.quantize_mx(out=K_codes[:, c, :].bitcast(E4), scales=K_scales[:, c, :], in_=flat(K_st[c]))

        sq, s_ps, rinv, U_ps, RI_ps, q, t_sb, o_sb = {}, {}, {}, {}, {}, {}, {}, {}

        def on_pe(n):
            return CFG["pe"][n]

        def squares(n):
            sq[n] = work.tile([P, D], F32, name="sq", tag="sq", bufs=2)
            nc.scalar.activation(sq[n][:], K_raw[n // 4][:, n % 4, :], ACT.Square)

        def sum_squares(n):
            if on_pe(n):
                s_ps[n] = psum.tile([P, F], F32, name="s_ps", tag="s_ps")
                nc.tensor.matmul(s_ps[n][:], lhsT=ident[:], rhs=sq[n][:, :F], start=True, stop=False)
                nc.tensor.matmul(s_ps[n][:], lhsT=ident[:], rhs=sq[n][:, F:], start=False, stop=True)
            else:
                s_ps[n] = work.tile([P, F], F32, name="s_sb", tag="s_sb", bufs=1)
                nc.vector.tensor_tensor(out=s_ps[n][:], in0=sq[n][:, :F], in1=sq[n][:, F:], op=ALU.add)

        def rsqrt(n):
            rinv[n] = work.tile([P, F], F32, name="rinv", tag="rinv", bufs=2)
            nc.scalar.activation(rinv[n][:], s_ps[n][:], ACT.Abs_reciprocal_sqrt, bias=EPS)

        def mm0(out, n, codes, scales):
            c, j = divmod(n, PACK)
            cols = slice(P * j, P * (j + 1))
            nc.tensor.matmul_mx(
                out=out[:],
                lhsT=gT_codes[c][:, cols].bitcast(E5),
                lhsT_scale=gT_scales[c][:, cols],
                rhs=codes.bitcast(E4),
                rhs_scale=scales,
                start=True,
                stop=True,
            )

        def U_mm(n):
            U_ps[n] = psum.tile([P, F], F32, name="U_ps", tag="U_ps")
            mm0(U_ps[n], n, u_codes[:], u_scales[:])

        def RI_mm(n):
            for h in range(2):
                RI_ps[n, h] = psum.tile([P, F], F32, name="RI_ps", tag="RI_ps", bufs=3)
                cols = slice(F * h, F * (h + 1))
                mm0(RI_ps[n, h], n, rot_codes[:, cols], rot_scales[:, cols])

        def q_mul(n):
            q[n] = work.tile([P, F], F32, name="q", tag="q", bufs=2)
            nc.vector.tensor_tensor(out=q[n][:], in0=U_ps[n][:], in1=rinv[n][:], op=ALU.mult)

        def t_mul(n):
            t_sb[n] = work.tile([P, 2, F], F32, name="t_sb", tag="t_sb", bufs=3)
            nc.gpsimd.tensor_tensor(
                out=t_sb[n][:],
                in0=q[n][:].unsqueeze(1).to_broadcast([P, 2, F]),
                in1=K_raw[n // 4][:, n % 4, :].rearrange("p (h f) -> p h f", h=2),
                op=ALU.mult,
            )

        def o_add(n):
            o_sb[n] = work.tile([P, 2, F], F32, name="o_sb", tag="o_sb", bufs=3)
            for h in range(2):
                nc.vector.tensor_tensor(out=o_sb[n][:, h, :], in0=RI_ps[n, h][:], in1=t_sb[n][:, h, :], op=ALU.add)
            nc.sync.dma_start(out=o0_hbm[:, n // 4, n % 4, :], in_=o_sb[n][:].rearrange("p h f -> p (h f)"))

        GT_ps, dpT, dp_ps, scaled = {}, {}, {}, {}

        def GT_mm(i, h):
            GT_ps[i, h] = psum.tile([P, B], F32, name="GT_ps", tag="G_ps", bufs=2)
            cols = slice(F * h + P * i, F * h + P * (i + 1))
            for c in range(NCHUNK):
                nc.tensor.matmul_mx(
                    out=GT_ps[i, h][:],
                    lhsT=K_codes[:, c, cols].bitcast(E4),
                    lhsT_scale=K_scales[:, c, cols],
                    rhs=g_codes[:, c, :].bitcast(E5),
                    rhs_scale=g_scales[:, c, :],
                    start=(c == 0),
                    stop=(c == NCHUNK - 1),
                )

        def GT_scale(i):
            scaled[i] = work.tile([P, 2, B], F32, name="scaled", tag="sq", bufs=2)
            for h in range(2):
                nc.scalar.activation(scaled[i][:, h, :], GT_ps[i, h][:], ACT.Copy, scale=c_col[:, i : i + 1])

        def GT_rotate(i):
            for h in range(2):
                if (i, h) == (0, 0) or (i, h) == (0, 1):
                    dpT[h] = work.tile([P, PACK, B], F32, name="dpT", tag="wide", bufs=CFG["kb"], align_bytes=64)
                nc.vector.scalar_tensor_tensor(
                    out=dpT[h][:, i, :], in0=GT_ps[i, 1 - h][:], scalar=(s_col, ns_col)[h][:, i : i + 1],
                    in1=scaled[i][:, h, :], op0=ALU.mult, op1=ALU.add)

        def dp_transpose(t):
            for h in range(2):
                dp_ps[t, h] = psum.tile([P, F], F32, name="dp_ps", tag="G_ps", bufs=2)
                for i in range(4):
                    nc.tensor.transpose(dp_ps[t, h][:, P * i : P * (i + 1)], dpT[h][:, i, P * t : P * (t + 1)], ident[:])

        x_sb = {}

        def dp_dot(t):
            junk = work.tile([P, 2, F], F32, name="junk", tag="o_sb", bufs=3)
            for h in range(2):
                nc.vector.scalar_tensor_tensor(
                    out=junk[:, h, :], in0=dp_ps[t, h][:], scalar=1.0, in1=probes_sb[:, t, F * h : F * (h + 1)],
                    op0=ALU.mult, op1=ALU.mult, accum_out=dots[:, 2 * t + h : 2 * t + h + 1])
            nc.vector.tensor_scalar(
                out=small[:, t : t + 1], in0=dots[:, 2 * t : 2 * t + 1],
                scalar1=dots[:, 2 * t + 1 : 2 * t + 2], scalar2=w_norm[:, t : t + 1], op0=ALU.add, op1=ALU.mult)
            x_sb[t] = work.tile([P, D], F32, name="x_sb", tag="sq", bufs=2)
            nc.scalar.activation(x_sb[t][:], probes_sb[:, t, :], ACT.Copy, scale=small[:, t : t + 1])

        def dp_final(t):
            o1 = work.tile([P, 2, F], F32, name="o1", tag="o_sb", bufs=3)
            for h in range(2):
                nc.vector.scalar_tensor_tensor(
                    out=o1[:, h, :], in0=dp_ps[t, h][:], scalar=r[:, t : t + 1], in1=x_sb[t][:, F * h : F * (h + 1)],
                    op0=ALU.mult, op1=ALU.add)
            nc.sync.dma_start(out=o1_hbm[:, t, :], in_=o1[:].rearrange("p h f -> p (h f)"))

        two_pi = 2.0 * math.pi
        k0 = work.tile([P, F], I32, name="k0", tag="q", bufs=2)
        k1 = work.tile([P, F], I32, name="k1", tag="q", bufs=2)
        ang = work.tile([P, 2, F], F32, name="ang", tag="t_sb", bufs=3)
        nc.vector.tensor_scalar(out=k0[:], in0=theta[:], scalar1=1.0 / two_pi, scalar2=None, op0=ALU.mult)
        nc.vector.tensor_scalar(out=k1[:], in0=theta[:], scalar1=1.0 / two_pi, scalar2=0.25, op0=ALU.mult, op1=ALU.add)
        nc.vector.scalar_tensor_tensor(out=ang[:, 0, :], in0=k0[:], scalar=-two_pi, in1=theta[:], op0=ALU.mult, op1=ALU.add)
        nc.vector.scalar_tensor_tensor(out=ang[:, 1, :], in0=k1[:], scalar=-two_pi, in1=theta[:], op0=ALU.mult, op1=ALU.add)
        nc.scalar.activation(sn[:], ang[:, 0, :], ACT.Sin)
        nc.scalar.activation(cs[:], ang[:, 1, :], ACT.Sin, bias=math.pi / 2.0)
        cs_ps = psum.tile([P, F], F32, name="cs_ps", tag="G_ps", bufs=2)
        sn_ps = psum.tile([P, F], F32, name="sn_ps", tag="G_ps", bufs=2)
        nc.tensor.matmul(sn_ps[:], lhsT=ident[:], rhs=sn[:], start=True, stop=True)
        nc.tensor.matmul(cs_ps[:], lhsT=ident[:], rhs=cs[:], start=True, stop=True)

        def columns(dst, src):
            ps = psum.tile([P, PACK, P], F32, name="col_ps", tag="xt")
            for i in range(PACK):
                nc.tensor.transpose(ps[:, i, :], src[:, P * i : P * (i + 1)], ident[:])
            nc.scalar.copy(out=dst[:].unsqueeze(2), in_=ps[:, :, 0:1])

        def tail_factors():
            columns(c_col, cs)
            columns(s_col, sn)
            nc.vector.tensor_scalar(out=ns_col[:], in0=s_col[:], scalar1=-1.0, scalar2=None, op0=ALU.mult)
            nc.vector.tensor_scalar(out=small[:], in0=r[:], scalar1=-EPS, scalar2=1.0, op0=ALU.mult, op1=ALU.add)
            nc.vector.tensor_tensor(out=w_norm[:], in0=r[:], in1=r[:], op=ALU.mult)
            nc.vector.reciprocal(small[:], small[:])
            nc.vector.tensor_tensor(out=w_norm[:], in0=w_norm[:], in1=r[:], op=ALU.mult)
            nc.vector.scalar_tensor_tensor(out=w_norm[:], in0=w_norm[:], scalar=-1.0, in1=small[:], op0=ALU.mult, op1=ALU.mult)

        def scaled_probes(jp):
            pr = work.tile([P, 2, D], F32, name="pr", tag="wide", bufs=CFG["kb"], align_bytes=64)
            for j in range(2):
                jj = 2 * jp + j
                nc.scalar.activation(pr[:, j, :], probes_sb[:, jj, :], ACT.Copy, scale=r[:, jj : jj + 1])
            return pr

        def rotate(jp, pr):
            js = slice(2 * jp, 2 * jp + 2)
            cb = cs_ps[:].unsqueeze(1).to_broadcast([P, 2, F])
            sb = sn_ps[:].unsqueeze(1).to_broadcast([P, 2, F])
            m = [work.tile([P, 2, F], F32, name="m", tag=tg, bufs=3) for tg in ("o_sb", "t_sb", "o_sb", "t_sb")]
            tt = nc.vector.tensor_tensor
            tt(out=m[0][:], in0=pr[:, :, :F], in1=cb, op=ALU.mult)
            tt(out=m[1][:], in0=pr[:, :, F:], in1=sb, op=ALU.mult)
            nc.gpsimd.tensor_tensor(out=rot_bf[:, js, :F], in0=m[0][:], in1=m[1][:], op=ALU.subtract)
            tt(out=m[2][:], in0=pr[:, :, F:], in1=cb, op=ALU.mult)
            tt(out=m[3][:], in0=pr[:, :, :F], in1=sb, op=ALU.mult)
            nc.gpsimd.tensor_tensor(out=rot_bf[:, js, F:], in0=m[2][:], in1=m[3][:], op=ALU.add)

        sc, vc = nc.scalar.copy, nc.vector.tensor_copy
        sk, sg, start = CFG["sk"], CFG["sg"], CFG["start"]

        def g_both(c):
            if sg[c] > 0:
                g_interleave(c, sc, 0, sg[c])
            if sg[c] < 4:
                g_interleave(c, vc, sg[c], 4)

        def K_part_s(c, a, b):
            if b > a:
                K_interleave(c, sc, a, b)

        def K_part_v(c):
            if sk[c] < 4:
                K_interleave(c, vc, sk[c], 4)

        pr0 = scaled_probes(0)
        g_transpose(0, 0)
        g_transpose_out(0, 0)
        g_transpose(0, 1)
        g_transpose_out(0, 1)
        g_both(0)
        u_st = work.tile([P, F, PACK], BF16, name="u_st", tag="gst", bufs=3, align_bytes=64)
        rotate(0, pr0)
        pr1 = scaled_probes(1)
        gT_quant(0)
        g_quant(0)
        interleave(sc if CFG["su"] else vc, u_st, u_raw, 0, F)
        rotate(1, pr1)
        nc.vector.quantize_mx(out=u_codes[:].bitcast(E4), scales=u_scales[:], in_=flat(u_st))
        squares(0)
        sum_squares(0)
        U_mm(0)
        squares(1)
        rot_st = work.tile([P, D, PACK], BF16, name="rot_st", tag="wide", bufs=CFG["kb"], align_bytes=64)
        K_part_v(0)
        if CFG["sr"]:
            interleave(sc, rot_st, rot_bf, D - 256 * CFG["sr"], D)
        interleave(vc, rot_st, rot_bf, 0, F)
        interleave(vc, rot_st, rot_bf, F, D - 256 * CFG["sr"])
        nc.vector.quantize_mx(out=rot_codes[:].bitcast(E4), scales=rot_scales[:], in_=flat(rot_st))

        plan_s, plan_v = {}, {}

        def put(plan, n, fn):
            plan.setdefault(n, []).append(fn)

        put(plan_s, 0, lambda: K_part_s(0, 0, sk[0]))
        put(plan_v, 1, lambda: K_quant(0))
        put(plan_v, 2, tail_factors)
        for c in range(1, NCHUNK):
            n = start[c]
            put(plan_s, n, lambda c=c: (g_transpose(c, 0), g_transpose_out(c, 0)))
            put(plan_s, n, lambda c=c: (g_transpose(c, 1), g_transpose_out(c, 1)))
            put(plan_v, n + 1, lambda c=c: gT_quant(c))
            put(plan_v, n + 1, lambda c=c: g_both(c))
            put(plan_s, n + 1, lambda c=c: K_part_s(c, 0, sk[c] // 2))
            put(plan_s, n + 2, lambda c=c: K_part_s(c, sk[c] // 2, sk[c]))
            put(plan_v, n + 2, lambda c=c: g_quant(c))
            put(plan_v, n + 2, lambda c=c: K_part_v(c))
            put(plan_v, n + 3, lambda c=c: K_quant(c))
        G0 = CFG["g0"]
        for i in range(4):
            n = G0 + (CFG["gs"] * i) // 2
            put(plan_v, n, lambda i=i: (GT_mm(i, 0), GT_mm(i, 1)))
            put(plan_s, n + 1, lambda i=i: GT_scale(i))
            put(plan_v, n + 1, lambda i=i: GT_rotate(i))
        for t in range(4):
            n = G0 + CFG["d0"] + t
            put(plan_v, n - 1, lambda t=t: dp_transpose(t))
            put(plan_v, n, lambda t=t: dp_dot(t))
            put(plan_v, n, lambda t=t: dp_final(t))

        for n in range(NTILE + 1):
            if n < NTILE:
                rsqrt(n)
                q_mul(n)
                t_mul(n)
            if n + 1 < NTILE:
                sum_squares(n + 1)
            for fn in plan_s.get(n, []):
                fn()
            if n + 2 < NTILE:
                squares(n + 2)
            if n >= 1:
                o_add(n - 1)
            if n + 1 < NTILE:
                U_mm(n + 1)
            if n < NTILE:
                RI_mm(n)
            for fn in plan_v.get(n, []):
                fn()
